import numpy as np
import ml_dtypes


def mxq(x, axis, fmt="e4m3"):
    dtype, down = {"e4m3": (ml_dtypes.float8_e4m3fn, 7), "e5m2": (ml_dtypes.float8_e5m2, 14)}[fmt]
    v = np.moveaxis(np.asarray(x, np.float32).astype(ml_dtypes.bfloat16).astype(np.float64), axis, -1)
    blocks = v.reshape(v.shape[:-1] + (-1, 32))
    amax = np.abs(blocks).max(-1, keepdims=True)
    byte = np.maximum(np.where(amax > 0, np.frexp(amax)[1] - 1 + 127, 0) - down, 1)
    scale = np.exp2(byte - 127.0)
    codes = (blocks / scale).astype(np.float32).astype(dtype).astype(np.float64)
    return np.moveaxis((codes * scale).reshape(v.shape), -1, axis)


WIDE = False


def mx_kscale(k):
    if not WIDE:
        return np.ones(k)
    levels = np.array([10, -10, 5, -5, 0])
    a = np.random.permutation(np.resize(levels, k // 512 * 4)).reshape(k // 512, 4)
    idx = np.arange(k)
    return np.exp2(a[idx // 512, idx % 128 // 32])


BF16 = ml_dtypes.bfloat16


def bf(x):
    return np.asarray(x, np.float32).astype(BF16)


def f64(x):
    return np.asarray(x).astype(np.float64)


B, N, F, FO, KC = 4, 512, 1024, 1024, 5


def setup_inputs():
    d = mx_kscale(N)
    d = d / d.max()
    a = np.random.standard_normal((N, N)) / np.sqrt(N)
    return {"z0": bf(np.random.standard_normal((B, N, F)) * d[:, None]),
            "z1": bf(0.7 * np.random.standard_normal((B, N, F)) * d[:, None]),
            "L": bf(0.5 * (a + a.T) * d[:, None] / d[None, :])}


def reference(z0, z1, L):
    z0, z1 = f64(z0), f64(z1)
    lq = mxq(f64(L), 1, "e4m3")
    z2 = 2.0 * (lq @ mxq(z1, 1, "e4m3")) - z0
    z3 = 2.0 * (lq @ mxq(z2, 1, "e4m3")) - z1
    return z2, z3

@@ -1,0 +1,170 @@
+from contextlib import ExitStack
+
+import concourse.mybir as mybir
+from concourse.masks import make_identity
+
+F32 = mybir.dt.float32
+BF16 = mybir.dt.bfloat16
+U32 = mybir.dt.uint32
+U8 = mybir.dt.uint8
+FP8X4 = mybir.dt.float8_e4m3fn_x4
+MULT = mybir.AluOpType.mult
+SUBTRACT = mybir.AluOpType.subtract
+
+P = 128
+PACK = 4
+B, N, F = 4, 512, 1024
+W = 512
+HALVES = F // W
+UNITS = B * HALVES
+FLOPS = 2 * 2 * B * N * N * F
+MANUAL = True
+
+
+def tile_manualchebconv_pb_kernel(tc, z0, z1, L, out_0, out_1):
+    nc = tc.nc
+    with ExitStack() as ctx:
+        if MANUAL:
+            ctx.enter_context(tc.manual_schedule())
+        const = ctx.enter_context(tc.tile_pool(name="const", bufs=1))
+        inputs = ctx.enter_context(tc.tile_pool(name="inputs", bufs=1))
+        grouped = ctx.enter_context(tc.tile_pool(name="grouped", bufs=3))
+        codes = ctx.enter_context(tc.tile_pool(name="codes", bufs=3))
+        results = ctx.enter_context(tc.tile_pool(name="results", bufs=5))
+        psum = ctx.enter_context(tc.psum_pool(name="psum", bufs=8))
+
+        def rows(dram, b):
+            return dram[b].rearrange("(p j) w -> p j w", j=PACK)
+
+        l_rows = const.tile([P, PACK * N], BF16)
+        nc.sync.dma_start(out=l_rows[:], in_=L.rearrange("(p j) m -> p (j m)", j=PACK))
+        z0_sb = []
+        z1_sb = []
+        for b in range(B):
+            cuts = HALVES if b == 0 else 1
+            width = F // cuts
+            for h in range(cuts):
+                for dram, views, name in ((z1, z1_sb, "z1"), (z0, z0_sb, "z0")):
+                    t = inputs.tile([P, PACK, width], BF16, name="%s_sb%d%d" % (name, b, h))
+                    nc.sync.dma_start(out=t[:], in_=rows(dram, b)[:, :, h * width : (h + 1) * width])
+                    views.extend([t[:, :, k * W : (k + 1) * W] for k in range(width // W)])
+
+        state = {}
+
+        def cols(u):
+            h = u % HALVES
+            return slice(h * W, (h + 1) * W)
+
+        def regroup(u, stage, src, copy):
+            g = grouped.tile([P, W, PACK], BF16, align_bytes=64, tag="g%d" % stage, name="g%d" % stage)
+            copy(
+                out=g[:].rearrange("p (c i) t -> p c t i", i=4),
+                in_=src.rearrange("p t (c i) -> p c t i", i=4),
+            )
+            state[("g", stage, u)] = g
+
+        def quantise(u, stage):
+            g = state[("g", stage, u)]
+            c = codes.tile([P, W], U32, align_bytes=64, tag="c%d" % stage, name="c%d" % stage)
+            s = codes.tile([P, W], U8, align_bytes=64, tag="s%d" % stage, name="s%d" % stage)
+            nc.vector.quantize_mx(
+                out=c[:].bitcast(FP8X4), scales=s[:], in_=g[:].rearrange("p w t -> p (w t)")
+            )
+            state[("q", stage, u)] = (c, s)
+
+        def multiply(u, stage):
+            c, s = state[("q", stage, u)]
+            banks = []
+            for j in range(PACK):
+                acc = psum.tile([P, W], F32, tag="bank", name="acc")
+                nc.tensor.matmul_mx(
+                    out=acc[:],
+                    lhsT=l_codes[:, j * P : (j + 1) * P].bitcast(FP8X4),
+                    lhsT_scale=l_scales[:, j * P : (j + 1) * P],
+                    rhs=c[:].bitcast(FP8X4),
+                    rhs_scale=s[:],
+                    start=True,
+                    stop=True,
+                )
+                banks.append(acc)
+            state[("acc", stage, u)] = banks
+
+        def finish(u, stage, j_lo, j_hi, older):
+            b = u // HALVES
+            if j_lo == 0:
+                if b == B - 1:
+                    zh = results.tile([P, PACK, W], F32, tag="zh", bufs=4)
+                    state[("z", stage, u)] = zh[:]
+                elif u % HALVES == 0:
+                    z_b = results.tile([P, PACK, F], F32, tag="z", name="z")
+                    state[("zb", stage, b)] = z_b
+                    for h in range(HALVES):
+                        state[("z", stage, u + h)] = z_b[:, :, h * W : (h + 1) * W]
+            z = state[("z", stage, u)]
+            for j in range(j_lo, j_hi):
+                nc.vector.scalar_tensor_tensor(
+                    out=z[:, j, :],
+                    in0=state[("acc", stage, u)][j][:],
+                    scalar=2.0,
+                    in1=older[u][:, j, :],
+                    op0=MULT,
+                    op1=SUBTRACT,
+                )
+
+        def store_part(u, stage, dram, j_part):
+            nc.sync.dma_start(
+                out=rows(dram, u // HALVES)[:, j_part, cols(u)], in_=state[("z", stage, u)][:, j_part, :]
+            )
+
+        def store_after(u, stage, dram):
+            b = u // HALVES
+            if b == B - 1:
+                store_part(u, stage, dram, slice(0, PACK))
+            elif u % HALVES == HALVES - 1:
+                nc.sync.dma_start(out=rows(dram, b), in_=state[("zb", stage, b)][:])
+
+        regroup(0, 1, z1_sb[0], nc.vector.tensor_copy)
+        quantise(0, 1)
+
+        ident = const.tile([P, P], F32)
+        make_identity(nc, ident[:])
+        l_words = l_rows[:].bitcast(F32).rearrange("p (j q u) -> p j u q", j=PACK, u=2)
+        l_grouped = const.tile([P, PACK * N], BF16, align_bytes=64)
+        l_grouped_words = l_grouped[:].bitcast(F32).rearrange("q (j p u) -> q j p u", j=PACK, u=2)
+        for pair in range(2):
+            l_t = psum.tile([P, 2, 2, P], F32, tag="bank")
+            for a in range(2):
+                for u in range(2):
+                    nc.tensor.transpose(l_t[:, a, u, :], l_words[:, 2 * pair + a, u, :], ident[:])
+            nc.scalar.copy(
+                out=l_grouped_words[:, 2 * pair : 2 * pair + 2, :, :],
+                in_=l_t[:].rearrange("q a u p -> q a p u"),
+            )
+        l_codes = const.tile([P, N], U32, align_bytes=64)
+        l_scales = const.tile([P, N], U8, align_bytes=64)
+        nc.vector.quantize_mx(out=l_codes[:].bitcast(FP8X4), scales=l_scales[:], in_=l_grouped[:])
+
+        regroup(1, 1, z1_sb[1], nc.scalar.copy)
+        multiply(0, 1)
+        for u in range(UNITS + 1):
+            if u < UNITS:
+                finish(u, 1, 0, 2, z0_sb)
+            if u >= 1:
+                quantise(u - 1, 2)
+                multiply(u - 1, 2)
+            if u < UNITS:
+                finish(u, 1, 2, PACK, z0_sb)
+                store_after(u, 1, out_0)
+                regroup(u, 2, state[("z", 1, u)], nc.scalar.copy)
+            if u + 2 < UNITS:
+                regroup(u + 2, 1, z1_sb[u + 2], nc.scalar.copy)
+            if u + 1 < UNITS:
+                quantise(u + 1, 1)
+                multiply(u + 1, 1)
+            if 1 <= u < UNITS:
+                finish(u - 1, 2, 0, PACK, z1_sb)
+                store_after(u - 1, 2, out_1)
+        last = UNITS - 1
+        for j in range(0, PACK, 2):
+            finish(last, 2, j, j + 2, z1_sb)
+            store_part(last, 2, out_1, slice(j, j + 2))

@@ -18,14 +18,13 @@ W = 512
 HALVES = F // W
 UNITS = B * HALVES
 FLOPS = 2 * 2 * B * N * N * F
-MANUAL = True
+OFFLOAD = True
 
 
 def tile_manualchebconv_pb_kernel(tc, z0, z1, L, out_0, out_1):
     nc = tc.nc
     with ExitStack() as ctx:
-        if MANUAL:
-            ctx.enter_context(tc.manual_schedule())
+        ctx.enter_context(tc.manual_schedule())
         const = ctx.enter_context(tc.tile_pool(name="const", bufs=1))
         inputs = ctx.enter_context(tc.tile_pool(name="inputs", bufs=1))
         grouped = ctx.enter_context(tc.tile_pool(name="grouped", bufs=3))
@@ -40,14 +39,19 @@ def tile_manualchebconv_pb_kernel(tc, z0, z1, L, out_0, out_1):
         nc.sync.dma_start(out=l_rows[:], in_=L.rearrange("(p j) m -> p (j m)", j=PACK))
         z0_sb = []
         z1_sb = []
-        for b in range(B):
-            cuts = HALVES if b == 0 else 1
-            width = F // cuts
-            for h in range(cuts):
-                for dram, views, name in ((z1, z1_sb, "z1"), (z0, z0_sb, "z0")):
-                    t = inputs.tile([P, PACK, width], BF16, name="%s_sb%d%d" % (name, b, h))
-                    nc.sync.dma_start(out=t[:], in_=rows(dram, b)[:, :, h * width : (h + 1) * width])
-                    views.extend([t[:, :, k * W : (k + 1) * W] for k in range(width // W)])
+        pieces = [(0, 0, W), (0, W, W)] + [(b, 0, F) for b in range(1, B)]
+
+        def load(dram, views, name, piece):
+            b, start, width = piece
+            t = inputs.tile([P, PACK, width], BF16, name="%s_sb%d_%d" % (name, b, start))
+            nc.sync.dma_start(out=t[:], in_=rows(dram, b)[:, :, start : start + width])
+            views.extend([t[:, :, k * W : (k + 1) * W] for k in range(width // W)])
+
+        load(z1, z1_sb, "z1", pieces[0])
+        for i in range(len(pieces)):
+            if i + 1 < len(pieces):
+                load(z1, z1_sb, "z1", pieces[i + 1])
+            load(z0, z0_sb, "z0", pieces[i])
 
         state = {}
 
@@ -72,10 +76,9 @@ def tile_manualchebconv_pb_kernel(tc, z0, z1, L, out_0, out_1):
             )
             state[("q", stage, u)] = (c, s)
 
-        def multiply(u, stage):
+        def multiply(u, stage, js):
             c, s = state[("q", stage, u)]
-            banks = []
-            for j in range(PACK):
+            for j in js:
                 acc = psum.tile([P, W], F32, tag="bank", name="acc")
                 nc.tensor.matmul_mx(
                     out=acc[:],
@@ -86,40 +89,45 @@ def tile_manualchebconv_pb_kernel(tc, z0, z1, L, out_0, out_1):
                     start=True,
                     stop=True,
                 )
-                banks.append(acc)
-            state[("acc", stage, u)] = banks
+                state[("acc", stage, u, j)] = acc
 
-        def finish(u, stage, j_lo, j_hi, older):
+        def in_halves(b, stage):
+            return b == B - 1 or (b == 0 and stage == 1)
+
+        def result(u, stage):
             b = u // HALVES
-            if j_lo == 0:
-                if b == B - 1:
+            if ("z", stage, u) not in state:
+                if in_halves(b, stage):
                     zh = results.tile([P, PACK, W], F32, tag="zh", bufs=4)
                     state[("z", stage, u)] = zh[:]
-                elif u % HALVES == 0:
-                    z_b = results.tile([P, PACK, F], F32, tag="z", name="z")
+                else:
+                    z_b = results.tile([P, PACK, F], F32, tag="z")
                     state[("zb", stage, b)] = z_b
                     for h in range(HALVES):
-                        state[("z", stage, u + h)] = z_b[:, :, h * W : (h + 1) * W]
-            z = state[("z", stage, u)]
-            for j in range(j_lo, j_hi):
+                        state[("z", stage, b * HALVES + h)] = z_b[:, :, h * W : (h + 1) * W]
+            return state[("z", stage, u)]
+
+        def finish(u, stage, js, older):
+            z = result(u, stage)
+            for j in js:
                 nc.vector.scalar_tensor_tensor(
                     out=z[:, j, :],
-                    in0=state[("acc", stage, u)][j][:],
+                    in0=state[("acc", stage, u, j)][:],
                     scalar=2.0,
                     in1=older[u][:, j, :],
                     op0=MULT,
                     op1=SUBTRACT,
                 )
 
-        def store_part(u, stage, dram, j_part):
-            nc.sync.dma_start(
-                out=rows(dram, u // HALVES)[:, j_part, cols(u)], in_=state[("z", stage, u)][:, j_part, :]
-            )
+        def finish_beside(u, stage, j, older):
+            z = result(u, stage)
+            nc.scalar.mul(out=z[:, j, :], in_=state[("acc", stage, u, j)][:], mul=2.0)
+            nc.gpsimd.tensor_tensor(out=z[:, j, :], in0=z[:, j, :], in1=older[u][:, j, :], op=SUBTRACT)
 
         def store_after(u, stage, dram):
             b = u // HALVES
-            if b == B - 1:
-                store_part(u, stage, dram, slice(0, PACK))
+            if in_halves(b, stage):
+                nc.sync.dma_start(out=rows(dram, b)[:, :, cols(u)], in_=state[("z", stage, u)])
             elif u % HALVES == HALVES - 1:
                 nc.sync.dma_start(out=rows(dram, b), in_=state[("zb", stage, b)][:])
 
@@ -134,8 +142,8 @@ def tile_manualchebconv_pb_kernel(tc, z0, z1, L, out_0, out_1):
         for pair in range(2):
             l_t = psum.tile([P, 2, 2, P], F32, tag="bank")
             for a in range(2):
-                for u in range(2):
-                    nc.tensor.transpose(l_t[:, a, u, :], l_words[:, 2 * pair + a, u, :], ident[:])
+                for e in range(2):
+                    nc.tensor.transpose(l_t[:, a, e, :], l_words[:, 2 * pair + a, e, :], ident[:])
             nc.scalar.copy(
                 out=l_grouped_words[:, 2 * pair : 2 * pair + 2, :, :],
                 in_=l_t[:].rearrange("q a u p -> q a p u"),
@@ -145,26 +153,27 @@ def tile_manualchebconv_pb_kernel(tc, z0, z1, L, out_0, out_1):
         nc.vector.quantize_mx(out=l_codes[:].bitcast(FP8X4), scales=l_scales[:], in_=l_grouped[:])
 
         regroup(1, 1, z1_sb[1], nc.scalar.copy)
-        multiply(0, 1)
-        for u in range(UNITS + 1):
+        multiply(0, 1, range(PACK))
+        for u in range(UNITS + 2):
             if u < UNITS:
-                finish(u, 1, 0, 2, z0_sb)
-            if u >= 1:
-                quantise(u - 1, 2)
-                multiply(u - 1, 2)
-            if u < UNITS:
-                finish(u, 1, 2, PACK, z0_sb)
+                finish(u, 1, range(PACK), z0_sb)
                 store_after(u, 1, out_0)
                 regroup(u, 2, state[("z", 1, u)], nc.scalar.copy)
-            if u + 2 < UNITS:
-                regroup(u + 2, 1, z1_sb[u + 2], nc.scalar.copy)
+            if 1 <= u <= UNITS:
+                quantise(u - 1, 2)
+                multiply(u - 1, 2, (0, 1))
             if u + 1 < UNITS:
                 quantise(u + 1, 1)
-                multiply(u + 1, 1)
-            if 1 <= u < UNITS:
-                finish(u - 1, 2, 0, PACK, z1_sb)
-                store_after(u - 1, 2, out_1)
-        last = UNITS - 1
-        for j in range(0, PACK, 2):
-            finish(last, 2, j, j + 2, z1_sb)
-            store_part(last, 2, out_1, slice(j, j + 2))
+                multiply(u + 1, 1, range(PACK))
+            if u >= 2:
+                finish(u - 2, 2, (2, 3), z1_sb)
+                store_after(u - 2, 2, out_1)
+            if 1 <= u <= UNITS:
+                multiply(u - 1, 2, (2, 3))
+                if OFFLOAD:
+                    finish_beside(u - 1, 2, 0, z1_sb)
+                    finish(u - 1, 2, (1,), z1_sb)
+                else:
+                    finish(u - 1, 2, (0, 1), z1_sb)
+            if u + 2 < UNITS:
+                regroup(u + 2, 1, z1_sb[u + 2], nc.scalar.copy)

@@ -29,7 +29,7 @@ def tile_manualchebconv_pb_kernel(tc, z0, z1, L, out_0, out_1):
         inputs = ctx.enter_context(tc.tile_pool(name="inputs", bufs=1))
         grouped = ctx.enter_context(tc.tile_pool(name="grouped", bufs=3))
         codes = ctx.enter_context(tc.tile_pool(name="codes", bufs=3))
-        results = ctx.enter_context(tc.tile_pool(name="results", bufs=5))
+        results = ctx.enter_context(tc.tile_pool(name="results", bufs=4))
         psum = ctx.enter_context(tc.psum_pool(name="psum", bufs=8))
 
         def rows(dram, b):
@@ -37,21 +37,18 @@ def tile_manualchebconv_pb_kernel(tc, z0, z1, L, out_0, out_1):
 
         l_rows = const.tile([P, PACK * N], BF16)
         nc.sync.dma_start(out=l_rows[:], in_=L.rearrange("(p j) m -> p (j m)", j=PACK))
-        z0_sb = []
-        z1_sb = []
-        pieces = [(0, 0, W), (0, W, W)] + [(b, 0, F) for b in range(1, B)]
 
-        def load(dram, views, name, piece):
-            b, start, width = piece
+        def load(dram, name, b, start, width):
             t = inputs.tile([P, PACK, width], BF16, name="%s_sb%d_%d" % (name, b, start))
             nc.sync.dma_start(out=t[:], in_=rows(dram, b)[:, :, start : start + width])
-            views.extend([t[:, :, k * W : (k + 1) * W] for k in range(width // W)])
+            return [t[:, :, k * W : (k + 1) * W] for k in range(width // W)]
 
-        load(z1, z1_sb, "z1", pieces[0])
-        for i in range(len(pieces)):
-            if i + 1 < len(pieces):
-                load(z1, z1_sb, "z1", pieces[i + 1])
-            load(z0, z0_sb, "z0", pieces[i])
+        z1_sb = load(z1, "z1", 0, 0, W)
+        z0_sb = load(z0, "z0", 0, 0, F)
+        z1_sb.extend(load(z1, "z1", 0, W, W))
+        for b in range(1, B):
+            z1_sb.extend(load(z1, "z1", b, 0, F))
+            z0_sb.extend(load(z0, "z0", b, 0, F))
 
         state = {}
 
@@ -91,20 +88,16 @@ def tile_manualchebconv_pb_kernel(tc, z0, z1, L, out_0, out_1):
                 )
                 state[("acc", stage, u, j)] = acc
 
-        def in_halves(b, stage):
-            return b == B - 1 or (b == 0 and stage == 1)
-
         def result(u, stage):
-            b = u // HALVES
             if ("z", stage, u) not in state:
-                if in_halves(b, stage):
-                    zh = results.tile([P, PACK, W], F32, tag="zh", bufs=4)
-                    state[("z", stage, u)] = zh[:]
+                if stage == 1:
+                    z2_u = results.tile([P, PACK, W], F32, tag="z2")
+                    state[("z", stage, u)] = z2_u[:]
                 else:
-                    z_b = results.tile([P, PACK, F], F32, tag="z")
-                    state[("zb", stage, b)] = z_b
+                    z3_b = results.tile([P, PACK, F], F32, tag="z3")
                     for h in range(HALVES):
-                        state[("z", stage, b * HALVES + h)] = z_b[:, :, h * W : (h + 1) * W]
+                        state[("z", stage, u + h)] = z3_b[:, :, h * W : (h + 1) * W]
+                    state[("z3", u // HALVES)] = z3_b
             return state[("z", stage, u)]
 
         def finish(u, stage, js, older):
@@ -124,12 +117,14 @@ def tile_manualchebconv_pb_kernel(tc, z0, z1, L, out_0, out_1):
             nc.scalar.mul(out=z[:, j, :], in_=state[("acc", stage, u, j)][:], mul=2.0)
             nc.gpsimd.tensor_tensor(out=z[:, j, :], in0=z[:, j, :], in1=older[u][:, j, :], op=SUBTRACT)
 
-        def store_after(u, stage, dram):
+        def store_z2(u):
+            nc.sync.dma_start(out=rows(out_0, u // HALVES)[:, :, cols(u)], in_=state[("z", 1, u)])
+
+        def store_z3(u, js):
             b = u // HALVES
-            if in_halves(b, stage):
-                nc.sync.dma_start(out=rows(dram, b)[:, :, cols(u)], in_=state[("z", stage, u)])
-            elif u % HALVES == HALVES - 1:
-                nc.sync.dma_start(out=rows(dram, b), in_=state[("zb", stage, b)][:])
+            if u % HALVES == HALVES - 1:
+                part = slice(js[0], js[-1] + 1)
+                nc.sync.dma_start(out=rows(out_1, b)[:, part, :], in_=state[("z3", b)][:, part, :])
 
         regroup(0, 1, z1_sb[0], nc.vector.tensor_copy)
         quantise(0, 1)
@@ -157,7 +152,7 @@ def tile_manualchebconv_pb_kernel(tc, z0, z1, L, out_0, out_1):
         for u in range(UNITS + 2):
             if u < UNITS:
                 finish(u, 1, range(PACK), z0_sb)
-                store_after(u, 1, out_0)
+                store_z2(u)
                 regroup(u, 2, state[("z", 1, u)], nc.scalar.copy)
             if 1 <= u <= UNITS:
                 quantise(u - 1, 2)
@@ -167,7 +162,7 @@ def tile_manualchebconv_pb_kernel(tc, z0, z1, L, out_0, out_1):
                 multiply(u + 1, 1, range(PACK))
             if u >= 2:
                 finish(u - 2, 2, (2, 3), z1_sb)
-                store_after(u - 2, 2, out_1)
+                store_z3(u - 2, (2, 3))
             if 1 <= u <= UNITS:
                 multiply(u - 1, 2, (2, 3))
                 if OFFLOAD:
@@ -175,5 +170,6 @@ def tile_manualchebconv_pb_kernel(tc, z0, z1, L, out_0, out_1):
                     finish(u - 1, 2, (1,), z1_sb)
                 else:
                     finish(u - 1, 2, (0, 1), z1_sb)
+                store_z3(u - 1, (0, 1))
             if u + 2 < UNITS:
                 regroup(u + 2, 1, z1_sb[u + 2], nc.scalar.copy)

@@ -16,9 +16,14 @@ PACK = 4
 B, N, F = 4, 512, 1024
 W = 512
 HALVES = F // W
-UNITS = B * HALVES
+BANKS = PACK * HALVES
 FLOPS = 2 * 2 * B * N * N * F
-OFFLOAD = True
+
+STEPS = ((1, 0), (1, 1), (1, 2), (2, 0), (1, 3), (2, 1), (2, 2), (2, 3))
+BY_HALF = tuple((j, h) for h in range(HALVES) for j in range(PACK))
+BY_ROW = tuple((j, h) for j in range(PACK) for h in range(HALVES))
+EARLY = 2
+BESIDE = (0, 4)
 
 
 def tile_manualchebconv_pb_kernel(tc, z0, z1, L, out_0, out_1):
@@ -27,9 +32,9 @@ def tile_manualchebconv_pb_kernel(tc, z0, z1, L, out_0, out_1):
         ctx.enter_context(tc.manual_schedule())
         const = ctx.enter_context(tc.tile_pool(name="const", bufs=1))
         inputs = ctx.enter_context(tc.tile_pool(name="inputs", bufs=1))
-        grouped = ctx.enter_context(tc.tile_pool(name="grouped", bufs=3))
-        codes = ctx.enter_context(tc.tile_pool(name="codes", bufs=3))
-        results = ctx.enter_context(tc.tile_pool(name="results", bufs=4))
+        grouped = ctx.enter_context(tc.tile_pool(name="grouped", bufs=4))
+        codes = ctx.enter_context(tc.tile_pool(name="codes", bufs=4))
+        results = ctx.enter_context(tc.tile_pool(name="results", bufs=3))
         psum = ctx.enter_context(tc.psum_pool(name="psum", bufs=8))
 
         def rows(dram, b):
@@ -37,45 +42,45 @@ def tile_manualchebconv_pb_kernel(tc, z0, z1, L, out_0, out_1):
 
         l_rows = const.tile([P, PACK * N], BF16)
         nc.sync.dma_start(out=l_rows[:], in_=L.rearrange("(p j) m -> p (j m)", j=PACK))
-
-        def load(dram, name, b, start, width):
-            t = inputs.tile([P, PACK, width], BF16, name="%s_sb%d_%d" % (name, b, start))
-            nc.sync.dma_start(out=t[:], in_=rows(dram, b)[:, :, start : start + width])
-            return [t[:, :, k * W : (k + 1) * W] for k in range(width // W)]
-
-        z1_sb = load(z1, "z1", 0, 0, W)
-        z0_sb = load(z0, "z0", 0, 0, F)
-        z1_sb.extend(load(z1, "z1", 0, W, W))
-        for b in range(1, B):
-            z1_sb.extend(load(z1, "z1", b, 0, F))
-            z0_sb.extend(load(z0, "z0", b, 0, F))
+        z1_sb = []
+        z0_sb = []
+        for b in range(B):
+            for dram, name, tiles in ((z1, "z1", z1_sb), (z0, "z0", z0_sb)):
+                t = inputs.tile([P, PACK, F], BF16, name="%s_sb%d" % (name, b))
+                nc.sync.dma_start(out=t[:], in_=rows(dram, b))
+                tiles.append(t)
+        older = {1: z0_sb, 2: z1_sb}
+        outs = {1: out_0, 2: out_1}
 
         state = {}
+        quantised = set()
+        emptied = set()
+        issued = [0]
 
-        def cols(u):
-            h = u % HALVES
+        def order(si):
+            return BY_HALF if si < EARLY else BY_ROW
+
+        all_banks = [STEPS[si] + jh for si in range(len(STEPS)) for jh in order(si)]
+
+        def cols(h):
             return slice(h * W, (h + 1) * W)
 
-        def regroup(u, stage, src, copy):
+        def regroup(stage, b, h, copy):
+            src = z1_sb[b] if stage == 1 else state[("z", 1, b)]
             g = grouped.tile([P, W, PACK], BF16, align_bytes=64, tag="g%d" % stage, name="g%d" % stage)
             copy(
                 out=g[:].rearrange("p (c i) t -> p c t i", i=4),
-                in_=src.rearrange("p t (c i) -> p c t i", i=4),
+                in_=src[:, :, cols(h)].rearrange("p t (c i) -> p c t i", i=4),
             )
-            state[("g", stage, u)] = g
+            state[("g", stage, b, h)] = g
 
-        def quantise(u, stage):
-            g = state[("g", stage, u)]
-            c = codes.tile([P, W], U32, align_bytes=64, tag="c%d" % stage, name="c%d" % stage)
-            s = codes.tile([P, W], U8, align_bytes=64, tag="s%d" % stage, name="s%d" % stage)
-            nc.vector.quantize_mx(
-                out=c[:].bitcast(FP8X4), scales=s[:], in_=g[:].rearrange("p w t -> p (w t)")
-            )
-            state[("q", stage, u)] = (c, s)
-
-        def multiply(u, stage, js):
-            c, s = state[("q", stage, u)]
-            for j in js:
+        def multiply_ready():
+            while issued[0] < len(all_banks):
+                n = issued[0]
+                stage, b, j, h = all_banks[n]
+                if (stage, b, h) not in quantised or (n >= BANKS and n - BANKS not in emptied):
+                    break
+                c, s = state[("q", stage, b, h)]
                 acc = psum.tile([P, W], F32, tag="bank", name="acc")
                 nc.tensor.matmul_mx(
                     out=acc[:],
@@ -86,48 +91,48 @@ def tile_manualchebconv_pb_kernel(tc, z0, z1, L, out_0, out_1):
                     start=True,
                     stop=True,
                 )
-                state[("acc", stage, u, j)] = acc
+                state[("acc", stage, b, j, h)] = acc
+                issued[0] = n + 1
 
-        def result(u, stage):
-            if ("z", stage, u) not in state:
-                if stage == 1:
-                    z2_u = results.tile([P, PACK, W], F32, tag="z2")
-                    state[("z", stage, u)] = z2_u[:]
-                else:
-                    z3_b = results.tile([P, PACK, F], F32, tag="z3")
-                    for h in range(HALVES):
-                        state[("z", stage, u + h)] = z3_b[:, :, h * W : (h + 1) * W]
-                    state[("z3", u // HALVES)] = z3_b
-            return state[("z", stage, u)]
+        def quantise(stage, b, h):
+            g = state[("g", stage, b, h)]
+            c = codes.tile([P, W], U32, align_bytes=64, tag="c%d" % stage, name="c%d" % stage)
+            s = codes.tile([P, W], U8, align_bytes=64, tag="s%d" % stage, name="s%d" % stage)
+            nc.vector.quantize_mx(
+                out=c[:].bitcast(FP8X4), scales=s[:], in_=g[:].rearrange("p w t -> p (w t)")
+            )
+            state[("q", stage, b, h)] = (c, s)
+            quantised.add((stage, b, h))
+            multiply_ready()
 
-        def finish(u, stage, js, older):
-            z = result(u, stage)
-            for j in js:
+        def result(stage, b):
+            if ("z", stage, b) not in state:
+                z = results.tile([P, PACK, F], F32, tag="res%d" % stage, name="res%d" % stage)
+                state[("z", stage, b)] = z
+            return state[("z", stage, b)]
+
+        def finish(stage, b, j, h, beside):
+            z = result(stage, b)
+            acc = state[("acc", stage, b, j, h)]
+            old = older[stage][b]
+            if beside:
+                nc.scalar.mul(out=z[:, j, cols(h)], in_=acc[:], mul=2.0)
+                nc.gpsimd.tensor_tensor(
+                    out=z[:, j, cols(h)], in0=z[:, j, cols(h)], in1=old[:, j, cols(h)], op=SUBTRACT
+                )
+            else:
                 nc.vector.scalar_tensor_tensor(
-                    out=z[:, j, :],
-                    in0=state[("acc", stage, u, j)][:],
+                    out=z[:, j, cols(h)],
+                    in0=acc[:],
                     scalar=2.0,
-                    in1=older[u][:, j, :],
+                    in1=old[:, j, cols(h)],
                     op0=MULT,
                     op1=SUBTRACT,
                 )
 
-        def finish_beside(u, stage, j, older):
-            z = result(u, stage)
-            nc.scalar.mul(out=z[:, j, :], in_=state[("acc", stage, u, j)][:], mul=2.0)
-            nc.gpsimd.tensor_tensor(out=z[:, j, :], in0=z[:, j, :], in1=older[u][:, j, :], op=SUBTRACT)
-
-        def store_z2(u):
-            nc.sync.dma_start(out=rows(out_0, u // HALVES)[:, :, cols(u)], in_=state[("z", 1, u)])
-
-        def store_z3(u, js):
-            b = u // HALVES
-            if u % HALVES == HALVES - 1:
-                part = slice(js[0], js[-1] + 1)
-                nc.sync.dma_start(out=rows(out_1, b)[:, part, :], in_=state[("z3", b)][:, part, :])
-
-        regroup(0, 1, z1_sb[0], nc.vector.tensor_copy)
-        quantise(0, 1)
+        def store(stage, b, first, count):
+            part = slice(first, first + count)
+            nc.sync.dma_start(out=rows(outs[stage], b)[:, part, :], in_=state[("z", stage, b)][:, part, :])
 
         ident = const.tile([P, P], F32)
         make_identity(nc, ident[:])
@@ -147,29 +152,33 @@ def tile_manualchebconv_pb_kernel(tc, z0, z1, L, out_0, out_1):
         l_scales = const.tile([P, N], U8, align_bytes=64)
         nc.vector.quantize_mx(out=l_codes[:].bitcast(FP8X4), scales=l_scales[:], in_=l_grouped[:])
 
-        regroup(1, 1, z1_sb[1], nc.scalar.copy)
-        multiply(0, 1, range(PACK))
-        for u in range(UNITS + 2):
-            if u < UNITS:
-                finish(u, 1, range(PACK), z0_sb)
-                store_z2(u)
-                regroup(u, 2, state[("z", 1, u)], nc.scalar.copy)
-            if 1 <= u <= UNITS:
-                quantise(u - 1, 2)
-                multiply(u - 1, 2, (0, 1))
-            if u + 1 < UNITS:
-                quantise(u + 1, 1)
-                multiply(u + 1, 1, range(PACK))
-            if u >= 2:
-                finish(u - 2, 2, (2, 3), z1_sb)
-                store_z3(u - 2, (2, 3))
-            if 1 <= u <= UNITS:
-                multiply(u - 1, 2, (2, 3))
-                if OFFLOAD:
-                    finish_beside(u - 1, 2, 0, z1_sb)
-                    finish(u - 1, 2, (1,), z1_sb)
-                else:
-                    finish(u - 1, 2, (0, 1), z1_sb)
-                store_z3(u - 1, (0, 1))
-            if u + 2 < UNITS:
-                regroup(u + 2, 1, z1_sb[u + 2], nc.scalar.copy)
+        due = {}
+        for si in range(len(STEPS)):
+            if si < EARLY:
+                places = ((si - 1, BANKS - 1), (si, 2))
+            else:
+                places = ((si - 1, BANKS - 2), (si - 1, BANKS - 1))
+            for h in range(HALVES):
+                due.setdefault(places[h], []).append(STEPS[si] + (h,))
+
+        regroup(1, 0, 0, nc.vector.tensor_copy)
+        regroup(1, 0, 1, nc.scalar.copy)
+        for stage, b, h in due[(-1, BANKS - 1)]:
+            quantise(stage, b, h)
+
+        for si in range(len(STEPS)):
+            stage, b = STEPS[si]
+            for i in range(BANKS):
+                j, h = order(si)[i]
+                if si + 1 < len(STEPS) and i % PACK == 0:
+                    regroup(STEPS[si + 1][0], STEPS[si + 1][1], i // PACK, nc.scalar.copy)
+                for q in due.get((si, i), []):
+                    quantise(q[0], q[1], q[2])
+                finish(stage, b, j, h, stage == 2 and i in BESIDE)
+                emptied.add(si * BANKS + i)
+                if si < EARLY:
+                    if i >= PACK and j % 2 == 1:
+                        store(stage, b, j - 1, 2)
+                elif j % 2 == 1 and h == HALVES - 1:
+                    store(stage, b, j - 1, 2)
+                multiply_ready()

@@ -23,7 +23,7 @@ STEPS = ((1, 0), (1, 1), (1, 2), (2, 0), (1, 3), (2, 1), (2, 2), (2, 3))
 BY_HALF = tuple((j, h) for h in range(HALVES) for j in range(PACK))
 BY_ROW = tuple((j, h) for j in range(PACK) for h in range(HALVES))
 EARLY = 2
-BESIDE = (0, 4)
+BESIDE = (4, 5)
 
 
 def tile_manualchebconv_pb_kernel(tc, z0, z1, L, out_0, out_1):
@@ -53,6 +53,8 @@ def tile_manualchebconv_pb_kernel(tc, z0, z1, L, out_0, out_1):
         outs = {1: out_0, 2: out_1}
 
         state = {}
+        doubled = []
+        fence = const.tile([P, 1], U32)
         quantised = set()
         emptied = set()
         issued = [0]
@@ -111,24 +113,30 @@ def tile_manualchebconv_pb_kernel(tc, z0, z1, L, out_0, out_1):
                 state[("z", stage, b)] = z
             return state[("z", stage, b)]
 
-        def finish(stage, b, j, h, beside):
-            z = result(stage, b)
-            acc = state[("acc", stage, b, j, h)]
-            old = older[stage][b]
-            if beside:
-                nc.scalar.mul(out=z[:, j, cols(h)], in_=acc[:], mul=2.0)
+        def finish(stage, b, j, h):
+            nc.vector.scalar_tensor_tensor(
+                out=result(stage, b)[:, j, cols(h)],
+                in0=state[("acc", stage, b, j, h)][:],
+                scalar=2.0,
+                in1=older[stage][b][:, j, cols(h)],
+                op0=MULT,
+                op1=SUBTRACT,
+            )
+
+        def double(stage, b, j, h):
+            nc.scalar.mul(out=result(stage, b)[:, j, cols(h)], in_=state[("acc", stage, b, j, h)][:], mul=2.0)
+            doubled.append((stage, b, j, h))
+
+        def subtract_doubled():
+            for stage, b, j, h in doubled:
+                z = result(stage, b)
                 nc.gpsimd.tensor_tensor(
-                    out=z[:, j, cols(h)], in0=z[:, j, cols(h)], in1=old[:, j, cols(h)], op=SUBTRACT
+                    out=z[:, j, cols(h)], in0=z[:, j, cols(h)], in1=older[stage][b][:, j, cols(h)], op=SUBTRACT
                 )
-            else:
-                nc.vector.scalar_tensor_tensor(
-                    out=z[:, j, cols(h)],
-                    in0=acc[:],
-                    scalar=2.0,
-                    in1=old[:, j, cols(h)],
-                    op0=MULT,
-                    op1=SUBTRACT,
-                )
+            doubled.clear()
+
+        def hold_gpsimd(stage, b, h):
+            nc.gpsimd.tensor_copy(out=fence[:], in_=state[("q", stage, b, h)][0][:, 0:1])
 
         def store(stage, b, first, count):
             part = slice(first, first + count)
@@ -156,8 +164,10 @@ def tile_manualchebconv_pb_kernel(tc, z0, z1, L, out_0, out_1):
         for si in range(len(STEPS)):
             if si < EARLY:
                 places = ((si - 1, BANKS - 1), (si, 2))
-            else:
+            elif si == EARLY:
                 places = ((si - 1, BANKS - 2), (si - 1, BANKS - 1))
+            else:
+                places = ((si - 1, BANKS - 3), (si - 1, BANKS - 2))
             for h in range(HALVES):
                 due.setdefault(places[h], []).append(STEPS[si] + (h,))
 
@@ -174,7 +184,15 @@ def tile_manualchebconv_pb_kernel(tc, z0, z1, L, out_0, out_1):
                     regroup(STEPS[si + 1][0], STEPS[si + 1][1], i // PACK, nc.scalar.copy)
                 for q in due.get((si, i), []):
                     quantise(q[0], q[1], q[2])
-                finish(stage, b, j, h, stage == 2 and i in BESIDE)
+                    if doubled and q[2] == HALVES - 1:
+                        hold_gpsimd(q[0], q[1], q[2])
+                        subtract_doubled()
+                if stage == 2 and i in BESIDE:
+                    double(stage, b, j, h)
+                    if si + 1 == len(STEPS):
+                        subtract_doubled()
+                else:
+                    finish(stage, b, j, h)
                 emptied.add(si * BANKS + i)
                 if si < EARLY:
                     if i >= PACK and j % 2 == 1:

@@ -197,6 +197,9 @@ def tile_manualchebconv_pb_kernel(tc, z0, z1, L, out_0, out_1):
                 if si < EARLY:
                     if i >= PACK and j % 2 == 1:
                         store(stage, b, j - 1, 2)
+                elif i == BANKS - 1 and stage == 2 and si + 1 < len(STEPS):
+                    store(stage, b, 3, 1)
+                    store(stage, b, 2, 1)
                 elif j % 2 == 1 and h == HALVES - 1:
                     store(stage, b, j - 1, 2)
                 multiply_ready()

@@ -23,6 +23,7 @@ STEPS = ((1, 0), (1, 1), (1, 2), (2, 0), (1, 3), (2, 1), (2, 2), (2, 3))
 BY_HALF = tuple((j, h) for h in range(HALVES) for j in range(PACK))
 BY_ROW = tuple((j, h) for j in range(PACK) for h in range(HALVES))
 EARLY = 2
+VECTOR_SHARE = 320
 BESIDE = (4, 5)
 
 
@@ -67,13 +68,14 @@ def tile_manualchebconv_pb_kernel(tc, z0, z1, L, out_0, out_1):
         def cols(h):
             return slice(h * W, (h + 1) * W)
 
-        def regroup(stage, b, h, copy):
+        def regroup(stage, b, h, shares):
             src = z1_sb[b] if stage == 1 else state[("z", 1, b)]
             g = grouped.tile([P, W, PACK], BF16, align_bytes=64, tag="g%d" % stage, name="g%d" % stage)
-            copy(
-                out=g[:].rearrange("p (c i) t -> p c t i", i=4),
-                in_=src[:, :, cols(h)].rearrange("p t (c i) -> p c t i", i=4),
-            )
+            for copy, first, count in shares:
+                copy(
+                    out=g[:, first : first + count, :].rearrange("p (c i) t -> p c t i", i=4),
+                    in_=src[:, :, h * W + first : h * W + first + count].rearrange("p t (c i) -> p c t i", i=4),
+                )
             state[("g", stage, b, h)] = g
 
         def multiply_ready():
@@ -147,6 +149,8 @@ def tile_manualchebconv_pb_kernel(tc, z0, z1, L, out_0, out_1):
         l_words = l_rows[:].bitcast(F32).rearrange("p (j q u) -> p j u q", j=PACK, u=2)
         l_grouped = const.tile([P, PACK * N], BF16, align_bytes=64)
         l_grouped_words = l_grouped[:].bitcast(F32).rearrange("q (j p u) -> q j p u", j=PACK, u=2)
+        l_codes = const.tile([P, N], U32, align_bytes=64)
+        l_scales = const.tile([P, N], U8, align_bytes=64)
         for pair in range(2):
             l_t = psum.tile([P, 2, 2, P], F32, tag="bank")
             for a in range(2):
@@ -156,9 +160,12 @@ def tile_manualchebconv_pb_kernel(tc, z0, z1, L, out_0, out_1):
                 out=l_grouped_words[:, 2 * pair : 2 * pair + 2, :, :],
                 in_=l_t[:].rearrange("q a u p -> q a p u"),
             )
-        l_codes = const.tile([P, N], U32, align_bytes=64)
-        l_scales = const.tile([P, N], U8, align_bytes=64)
-        nc.vector.quantize_mx(out=l_codes[:].bitcast(FP8X4), scales=l_scales[:], in_=l_grouped[:])
+            part = slice(2 * pair * P, 2 * (pair + 1) * P)
+            nc.vector.quantize_mx(
+                out=l_codes[:, part].bitcast(FP8X4),
+                scales=l_scales[:, part],
+                in_=l_grouped[:, 2 * pair * P * PACK : 2 * (pair + 1) * P * PACK],
+            )
 
         due = {}
         for si in range(len(STEPS)):
@@ -171,8 +178,10 @@ def tile_manualchebconv_pb_kernel(tc, z0, z1, L, out_0, out_1):
             for h in range(HALVES):
                 due.setdefault(places[h], []).append(STEPS[si] + (h,))
 
-        regroup(1, 0, 0, nc.vector.tensor_copy)
-        regroup(1, 0, 1, nc.scalar.copy)
+        regroup(
+            1, 0, 0, ((nc.vector.tensor_copy, 0, VECTOR_SHARE), (nc.scalar.copy, VECTOR_SHARE, W - VECTOR_SHARE))
+        )
+        regroup(1, 0, 1, ((nc.scalar.copy, 0, W),))
         for stage, b, h in due[(-1, BANKS - 1)]:
             quantise(stage, b, h)
 
@@ -181,7 +190,7 @@ def tile_manualchebconv_pb_kernel(tc, z0, z1, L, out_0, out_1):
             for i in range(BANKS):
                 j, h = order(si)[i]
                 if si + 1 < len(STEPS) and i % PACK == 0:
-                    regroup(STEPS[si + 1][0], STEPS[si + 1][1], i // PACK, nc.scalar.copy)
+                    regroup(STEPS[si + 1][0], STEPS[si + 1][1], i // PACK, ((nc.scalar.copy, 0, W),))
                 for q in due.get((si, i), []):
                     quantise(q[0], q[1], q[2])
                     if doubled and q[2] == HALVES - 1:

@@ -23,6 +23,7 @@ STEPS = ((1, 0), (1, 1), (1, 2), (2, 0), (1, 3), (2, 1), (2, 2), (2, 3))
 BY_HALF = tuple((j, h) for h in range(HALVES) for j in range(PACK))
 BY_ROW = tuple((j, h) for j in range(PACK) for h in range(HALVES))
 EARLY = 2
+WHOLE = 3
 VECTOR_SHARE = 320
 BESIDE = (4, 5)
 
@@ -203,9 +204,9 @@ def tile_manualchebconv_pb_kernel(tc, z0, z1, L, out_0, out_1):
                 else:
                     finish(stage, b, j, h)
                 emptied.add(si * BANKS + i)
-                if si < EARLY:
-                    if i >= PACK and j % 2 == 1:
-                        store(stage, b, j - 1, 2)
+                if si < WHOLE:
+                    if i == BANKS - 1:
+                        store(stage, b, 0, PACK)
                 elif i == BANKS - 1 and stage == 2 and si + 1 < len(STEPS):
                     store(stage, b, 3, 1)
                     store(stage, b, 2, 1)

@@ -24,6 +24,7 @@ BY_HALF = tuple((j, h) for h in range(HALVES) for j in range(PACK))
 BY_ROW = tuple((j, h) for j in range(PACK) for h in range(HALVES))
 EARLY = 2
 WHOLE = 3
+EARLY_LOADS = 5
 VECTOR_SHARE = 320
 BESIDE = (4, 5)
 
@@ -46,10 +47,14 @@ def tile_manualchebconv_pb_kernel(tc, z0, z1, L, out_0, out_1):
         nc.sync.dma_start(out=l_rows[:], in_=L.rearrange("(p j) m -> p (j m)", j=PACK))
         z1_sb = []
         z0_sb = []
+        late_loads = []
         for b in range(B):
             for dram, name, tiles in ((z1, "z1", z1_sb), (z0, "z0", z0_sb)):
                 t = inputs.tile([P, PACK, F], BF16, name="%s_sb%d" % (name, b))
-                nc.sync.dma_start(out=t[:], in_=rows(dram, b))
+                if len(z1_sb) + len(z0_sb) < EARLY_LOADS:
+                    nc.sync.dma_start(out=t[:], in_=rows(dram, b))
+                else:
+                    late_loads.append((t, dram, b))
                 tiles.append(t)
         older = {1: z0_sb, 2: z1_sb}
         outs = {1: out_0, 2: out_1}
@@ -192,6 +197,9 @@ def tile_manualchebconv_pb_kernel(tc, z0, z1, L, out_0, out_1):
                 j, h = order(si)[i]
                 if si + 1 < len(STEPS) and i % PACK == 0:
                     regroup(STEPS[si + 1][0], STEPS[si + 1][1], i // PACK, ((nc.scalar.copy, 0, W),))
+                    for t, dram, late_b in late_loads:
+                        nc.scalar.dma_start(out=t[:], in_=rows(dram, late_b))
+                    late_loads.clear()
                 for q in due.get((si, i), []):
                     quantise(q[0], q[1], q[2])
                     if doubled and q[2] == HALVES - 1:

@@ -24,7 +24,6 @@ BY_HALF = tuple((j, h) for h in range(HALVES) for j in range(PACK))
 BY_ROW = tuple((j, h) for j in range(PACK) for h in range(HALVES))
 EARLY = 2
 WHOLE = 3
-EARLY_LOADS = 5
 VECTOR_SHARE = 320
 BESIDE = (4, 5)
 
@@ -43,20 +42,35 @@ def tile_manualchebconv_pb_kernel(tc, z0, z1, L, out_0, out_1):
         def rows(dram, b):
             return dram[b].rearrange("(p j) w -> p j w", j=PACK)
 
-        l_rows = const.tile([P, PACK * N], BF16)
-        nc.sync.dma_start(out=l_rows[:], in_=L.rearrange("(p j) m -> p (j m)", j=PACK))
-        z1_sb = []
-        z0_sb = []
-        late_loads = []
-        for b in range(B):
-            for dram, name, tiles in ((z1, "z1", z1_sb), (z0, "z0", z0_sb)):
-                t = inputs.tile([P, PACK, F], BF16, name="%s_sb%d" % (name, b))
-                if len(z1_sb) + len(z0_sb) < EARLY_LOADS:
-                    nc.sync.dma_start(out=t[:], in_=rows(dram, b))
-                else:
-                    late_loads.append((t, dram, b))
-                tiles.append(t)
-        older = {1: z0_sb, 2: z1_sb}
+        l_rows = []
+        halves = {}
+
+        def load_l(pair):
+            t = const.tile([P, 2, N], BF16, name="l_rows%d" % pair)
+            nc.sync.dma_start(out=t[:], in_=L.rearrange("(p j) m -> p j m", j=PACK)[:, 2 * pair : 2 * pair + 2, :])
+            l_rows.append(t)
+
+        def load_half(dram, name, h):
+            t = inputs.tile([P, PACK, W], BF16, name="%s_half%d" % (name, h))
+            nc.sync.dma_start(out=t[:], in_=rows(dram, 0)[:, :, h * W : (h + 1) * W])
+            halves[(name, 0, h)] = t[:]
+
+        def load_whole(dram, name, b):
+            t = inputs.tile([P, PACK, F], BF16, name="%s_sb%d" % (name, b))
+            nc.sync.dma_start(out=t[:], in_=rows(dram, b))
+            for h in range(HALVES):
+                halves[(name, b, h)] = t[:, :, h * W : (h + 1) * W]
+
+        load_l(0)
+        load_half(z1, "z1", 0)
+        load_l(1)
+        load_half(z0, "z0", 0)
+        load_half(z1, "z1", 1)
+        load_half(z0, "z0", 1)
+        for b in range(1, B):
+            load_whole(z1, "z1", b)
+            load_whole(z0, "z0", b)
+        older = {1: "z0", 2: "z1"}
         outs = {1: out_0, 2: out_1}
 
         state = {}
@@ -75,12 +89,12 @@ def tile_manualchebconv_pb_kernel(tc, z0, z1, L, out_0, out_1):
             return slice(h * W, (h + 1) * W)
 
         def regroup(stage, b, h, shares):
-            src = z1_sb[b] if stage == 1 else state[("z", 1, b)]
+            src = halves[("z1", b, h)] if stage == 1 else state[("z", 1, b)][:, :, cols(h)]
             g = grouped.tile([P, W, PACK], BF16, align_bytes=64, tag="g%d" % stage, name="g%d" % stage)
             for copy, first, count in shares:
                 copy(
                     out=g[:, first : first + count, :].rearrange("p (c i) t -> p c t i", i=4),
-                    in_=src[:, :, h * W + first : h * W + first + count].rearrange("p t (c i) -> p c t i", i=4),
+                    in_=src[:, :, first : first + count].rearrange("p t (c i) -> p c t i", i=4),
                 )
             state[("g", stage, b, h)] = g
 
@@ -126,7 +140,7 @@ def tile_manualchebconv_pb_kernel(tc, z0, z1, L, out_0, out_1):
                 out=result(stage, b)[:, j, cols(h)],
                 in0=state[("acc", stage, b, j, h)][:],
                 scalar=2.0,
-                in1=older[stage][b][:, j, cols(h)],
+                in1=halves[(older[stage], b, h)][:, j, :],
                 op0=MULT,
                 op1=SUBTRACT,
             )
@@ -139,7 +153,7 @@ def tile_manualchebconv_pb_kernel(tc, z0, z1, L, out_0, out_1):
             for stage, b, j, h in doubled:
                 z = result(stage, b)
                 nc.gpsimd.tensor_tensor(
-                    out=z[:, j, cols(h)], in0=z[:, j, cols(h)], in1=older[stage][b][:, j, cols(h)], op=SUBTRACT
+                    out=z[:, j, cols(h)], in0=z[:, j, cols(h)], in1=halves[(older[stage], b, h)][:, j, :], op=SUBTRACT
                 )
             doubled.clear()
 
@@ -152,20 +166,23 @@ def tile_manualchebconv_pb_kernel(tc, z0, z1, L, out_0, out_1):
 
         ident = const.tile([P, P], F32)
         make_identity(nc, ident[:])
-        l_words = l_rows[:].bitcast(F32).rearrange("p (j q u) -> p j u q", j=PACK, u=2)
         l_grouped = const.tile([P, PACK * N], BF16, align_bytes=64)
         l_grouped_words = l_grouped[:].bitcast(F32).rearrange("q (j p u) -> q j p u", j=PACK, u=2)
         l_codes = const.tile([P, N], U32, align_bytes=64)
         l_scales = const.tile([P, N], U8, align_bytes=64)
+        first_shares = ((nc.vector.tensor_copy, 0, VECTOR_SHARE), (nc.scalar.copy, VECTOR_SHARE, W - VECTOR_SHARE))
         for pair in range(2):
+            l_words = l_rows[pair][:].bitcast(F32).rearrange("p j (q u) -> p j u q", u=2)
             l_t = psum.tile([P, 2, 2, P], F32, tag="bank")
             for a in range(2):
                 for e in range(2):
-                    nc.tensor.transpose(l_t[:, a, e, :], l_words[:, 2 * pair + a, e, :], ident[:])
+                    nc.tensor.transpose(l_t[:, a, e, :], l_words[:, a, e, :], ident[:])
             nc.scalar.copy(
                 out=l_grouped_words[:, 2 * pair : 2 * pair + 2, :, :],
                 in_=l_t[:].rearrange("q a u p -> q a p u"),
             )
+            if pair == 0:
+                regroup(1, 0, 0, first_shares)
             part = slice(2 * pair * P, 2 * (pair + 1) * P)
             nc.vector.quantize_mx(
                 out=l_codes[:, part].bitcast(FP8X4),
@@ -175,7 +192,9 @@ def tile_manualchebconv_pb_kernel(tc, z0, z1, L, out_0, out_1):
 
         due = {}
         for si in range(len(STEPS)):
-            if si < EARLY:
+            if si == 0:
+                places = ((-1, BANKS - 1), (0, PACK - 1))
+            elif si < EARLY:
                 places = ((si - 1, BANKS - 1), (si, 2))
             elif si == EARLY:
                 places = ((si - 1, BANKS - 2), (si - 1, BANKS - 1))
@@ -184,9 +203,6 @@ def tile_manualchebconv_pb_kernel(tc, z0, z1, L, out_0, out_1):
             for h in range(HALVES):
                 due.setdefault(places[h], []).append(STEPS[si] + (h,))
 
-        regroup(
-            1, 0, 0, ((nc.vector.tensor_copy, 0, VECTOR_SHARE), (nc.scalar.copy, VECTOR_SHARE, W - VECTOR_SHARE))
-        )
         regroup(1, 0, 1, ((nc.scalar.copy, 0, W),))
         for stage, b, h in due[(-1, BANKS - 1)]:
             quantise(stage, b, h)
@@ -197,9 +213,6 @@ def tile_manualchebconv_pb_kernel(tc, z0, z1, L, out_0, out_1):
                 j, h = order(si)[i]
                 if si + 1 < len(STEPS) and i % PACK == 0:
                     regroup(STEPS[si + 1][0], STEPS[si + 1][1], i // PACK, ((nc.scalar.copy, 0, W),))
-                    for t, dram, late_b in late_loads:
-                        nc.scalar.dma_start(out=t[:], in_=rows(dram, late_b))
-                    late_loads.clear()
                 for q in due.get((si, i), []):
                     quantise(q[0], q[1], q[2])
                     if doubled and q[2] == HALVES - 1:

@@ -24,6 +24,7 @@ BY_HALF = tuple((j, h) for h in range(HALVES) for j in range(PACK))
 BY_ROW = tuple((j, h) for j in range(PACK) for h in range(HALVES))
 EARLY = 2
 WHOLE = 3
+VECTOR_SHARE_1 = 128
 VECTOR_SHARE = 320
 BESIDE = (4, 5)
 
@@ -66,8 +67,10 @@ def tile_manualchebconv_pb_kernel(tc, z0, z1, L, out_0, out_1):
         load_l(1)
         load_half(z0, "z0", 0)
         load_half(z1, "z1", 1)
+        load_whole(z1, "z1", 1)
         load_half(z0, "z0", 1)
-        for b in range(1, B):
+        load_whole(z0, "z0", 1)
+        for b in range(2, B):
             load_whole(z1, "z1", b)
             load_whole(z0, "z0", b)
         older = {1: "z0", 2: "z1"}
@@ -77,6 +80,7 @@ def tile_manualchebconv_pb_kernel(tc, z0, z1, L, out_0, out_1):
         doubled = []
         fence = const.tile([P, 1], U32)
         quantised = set()
+        l_quantised = set()
         emptied = set()
         issued = [0]
 
@@ -90,19 +94,21 @@ def tile_manualchebconv_pb_kernel(tc, z0, z1, L, out_0, out_1):
 
         def regroup(stage, b, h, shares):
             src = halves[("z1", b, h)] if stage == 1 else state[("z", 1, b)][:, :, cols(h)]
-            g = grouped.tile([P, W, PACK], BF16, align_bytes=64, tag="g%d" % stage, name="g%d" % stage)
+            if ("g", stage, b, h) not in state:
+                g = grouped.tile([P, W, PACK], BF16, align_bytes=64, tag="g%d" % stage, name="g%d" % stage)
+                state[("g", stage, b, h)] = g
+            g = state[("g", stage, b, h)]
             for copy, first, count in shares:
                 copy(
                     out=g[:, first : first + count, :].rearrange("p (c i) t -> p c t i", i=4),
                     in_=src[:, :, first : first + count].rearrange("p t (c i) -> p c t i", i=4),
                 )
-            state[("g", stage, b, h)] = g
 
         def multiply_ready():
             while issued[0] < len(all_banks):
                 n = issued[0]
                 stage, b, j, h = all_banks[n]
-                if (stage, b, h) not in quantised or (n >= BANKS and n - BANKS not in emptied):
+                if j // 2 not in l_quantised or (stage, b, h) not in quantised or (n >= BANKS and n - BANKS not in emptied):
                     break
                 c, s = state[("q", stage, b, h)]
                 acc = psum.tile([P, W], F32, tag="bank", name="acc")
@@ -170,8 +176,8 @@ def tile_manualchebconv_pb_kernel(tc, z0, z1, L, out_0, out_1):
         l_grouped_words = l_grouped[:].bitcast(F32).rearrange("q (j p u) -> q j p u", j=PACK, u=2)
         l_codes = const.tile([P, N], U32, align_bytes=64)
         l_scales = const.tile([P, N], U8, align_bytes=64)
-        first_shares = ((nc.vector.tensor_copy, 0, VECTOR_SHARE), (nc.scalar.copy, VECTOR_SHARE, W - VECTOR_SHARE))
-        for pair in range(2):
+
+        def transpose_l(pair):
             l_words = l_rows[pair][:].bitcast(F32).rearrange("p j (q u) -> p j u q", u=2)
             l_t = psum.tile([P, 2, 2, P], F32, tag="bank")
             for a in range(2):
@@ -181,19 +187,21 @@ def tile_manualchebconv_pb_kernel(tc, z0, z1, L, out_0, out_1):
                 out=l_grouped_words[:, 2 * pair : 2 * pair + 2, :, :],
                 in_=l_t[:].rearrange("q a u p -> q a p u"),
             )
-            if pair == 0:
-                regroup(1, 0, 0, first_shares)
+
+        def quantise_l(pair):
             part = slice(2 * pair * P, 2 * (pair + 1) * P)
             nc.vector.quantize_mx(
                 out=l_codes[:, part].bitcast(FP8X4),
                 scales=l_scales[:, part],
                 in_=l_grouped[:, 2 * pair * P * PACK : 2 * (pair + 1) * P * PACK],
             )
+            l_quantised.add(pair)
+            multiply_ready()
 
         due = {}
         for si in range(len(STEPS)):
             if si == 0:
-                places = ((-1, BANKS - 1), (0, PACK - 1))
+                places = (None, (0, PACK - 1))
             elif si < EARLY:
                 places = ((si - 1, BANKS - 1), (si, 2))
             elif si == EARLY:
@@ -203,9 +211,15 @@ def tile_manualchebconv_pb_kernel(tc, z0, z1, L, out_0, out_1):
             for h in range(HALVES):
                 due.setdefault(places[h], []).append(STEPS[si] + (h,))
 
-        regroup(1, 0, 1, ((nc.scalar.copy, 0, W),))
-        for stage, b, h in due[(-1, BANKS - 1)]:
-            quantise(stage, b, h)
+        transpose_l(0)
+        regroup(
+            1, 0, 0, ((nc.vector.tensor_copy, 0, VECTOR_SHARE), (nc.scalar.copy, VECTOR_SHARE, W - VECTOR_SHARE))
+        )
+        quantise_l(0)
+        transpose_l(1)
+        quantise(1, 0, 0)
+        quantise_l(1)
+        regroup(1, 0, 1, ((nc.scalar.copy, VECTOR_SHARE_1, W - VECTOR_SHARE_1),))
 
         for si in range(len(STEPS)):
             stage, b = STEPS[si]
@@ -213,6 +227,8 @@ def tile_manualchebconv_pb_kernel(tc, z0, z1, L, out_0, out_1):
                 j, h = order(si)[i]
                 if si + 1 < len(STEPS) and i % PACK == 0:
                     regroup(STEPS[si + 1][0], STEPS[si + 1][1], i // PACK, ((nc.scalar.copy, 0, W),))
+                if (si, i) == (0, 2):
+                    regroup(1, 0, 1, ((nc.vector.tensor_copy, 0, VECTOR_SHARE_1),))
                 for q in due.get((si, i), []):
                     quantise(q[0], q[1], q[2])
                     if doubled and q[2] == HALVES - 1:
@@ -225,12 +241,9 @@ def tile_manualchebconv_pb_kernel(tc, z0, z1, L, out_0, out_1):
                 else:
                     finish(stage, b, j, h)
                 emptied.add(si * BANKS + i)
-                if si < WHOLE:
+                if stage == 1:
                     if i == BANKS - 1:
                         store(stage, b, 0, PACK)
-                elif i == BANKS - 1 and stage == 2 and si + 1 < len(STEPS):
-                    store(stage, b, 3, 1)
-                    store(stage, b, 2, 1)
                 elif j % 2 == 1 and h == HALVES - 1:
                     store(stage, b, j - 1, 2)
                 multiply_ready()

@@ -47,17 +47,17 @@ def tile_manualchebconv_pb_kernel(tc, z0, z1, L, out_0, out_1):
         halves = {}
 
         def load_l(pair):
-            t = const.tile([P, 2, N], BF16, name="l_rows%d" % pair)
+            t = const.tile([P, 2, N], BF16, align_bytes=256, name="l_rows%d" % pair)
             nc.sync.dma_start(out=t[:], in_=L.rearrange("(p j) m -> p j m", j=PACK)[:, 2 * pair : 2 * pair + 2, :])
             l_rows.append(t)
 
         def load_half(dram, name, h):
-            t = inputs.tile([P, PACK, W], BF16, name="%s_half%d" % (name, h))
+            t = inputs.tile([P, PACK, W], BF16, align_bytes=256, name="%s_half%d" % (name, h))
             nc.sync.dma_start(out=t[:], in_=rows(dram, 0)[:, :, h * W : (h + 1) * W])
             halves[(name, 0, h)] = t[:]
 
         def load_whole(dram, name, b):
-            t = inputs.tile([P, PACK, F], BF16, name="%s_sb%d" % (name, b))
+            t = inputs.tile([P, PACK, F], BF16, align_bytes=256, name="%s_sb%d" % (name, b))
             nc.sync.dma_start(out=t[:], in_=rows(dram, b))
             for h in range(HALVES):
                 halves[(name, b, h)] = t[:, :, h * W : (h + 1) * W]
@@ -137,7 +137,7 @@ def tile_manualchebconv_pb_kernel(tc, z0, z1, L, out_0, out_1):
 
         def result(stage, b):
             if ("z", stage, b) not in state:
-                z = results.tile([P, PACK, F], F32, tag="res%d" % stage, name="res%d" % stage)
+                z = results.tile([P, PACK, F], F32, align_bytes=256, tag="res%d" % stage, name="res%d" % stage)
                 state[("z", stage, b)] = z
             return state[("z", stage, b)]
 

from contextlib import ExitStack

import concourse.mybir as mybir
from concourse.masks import make_identity

F32 = mybir.dt.float32
BF16 = mybir.dt.bfloat16
U32 = mybir.dt.uint32
U8 = mybir.dt.uint8
FP8X4 = mybir.dt.float8_e4m3fn_x4
MULT = mybir.AluOpType.mult
SUBTRACT = mybir.AluOpType.subtract

P = 128
PACK = 4
B, N, F = 4, 512, 1024
W = 512
HALVES = F // W
BANKS = PACK * HALVES
FLOPS = 2 * 2 * B * N * N * F

STEPS = ((1, 0), (1, 1), (1, 2), (2, 0), (1, 3), (2, 1), (2, 2), (2, 3))
BY_HALF = tuple((j, h) for h in range(HALVES) for j in range(PACK))
BY_ROW = tuple((j, h) for j in range(PACK) for h in range(HALVES))
EARLY = 2
WHOLE = 3
VECTOR_SHARE_1 = 128
VECTOR_SHARE = 320
BESIDE = (4, 5)


def tile_manualchebconv_pb_kernel(tc, z0, z1, L, out_0, out_1):
    nc = tc.nc
    with ExitStack() as ctx:
        ctx.enter_context(tc.manual_schedule())
        const = ctx.enter_context(tc.tile_pool(name="const", bufs=1))
        inputs = ctx.enter_context(tc.tile_pool(name="inputs", bufs=1))
        grouped = ctx.enter_context(tc.tile_pool(name="grouped", bufs=4))
        codes = ctx.enter_context(tc.tile_pool(name="codes", bufs=4))
        results = ctx.enter_context(tc.tile_pool(name="results", bufs=3))
        psum = ctx.enter_context(tc.psum_pool(name="psum", bufs=8))

        def rows(dram, b):
            return dram[b].rearrange("(p j) w -> p j w", j=PACK)

        l_rows = []
        halves = {}

        def load_l(pair):
            t = const.tile([P, 2, N], BF16, align_bytes=256, name="l_rows%d" % pair)
            nc.sync.dma_start(out=t[:], in_=L.rearrange("(p j) m -> p j m", j=PACK)[:, 2 * pair : 2 * pair + 2, :])
            l_rows.append(t)

        def load_half(dram, name, h):
            t = inputs.tile([P, PACK, W], BF16, align_bytes=256, name="%s_half%d" % (name, h))
            nc.sync.dma_start(out=t[:], in_=rows(dram, 0)[:, :, h * W : (h + 1) * W])
            halves[(name, 0, h)] = t[:]

        def load_whole(dram, name, b):
            t = inputs.tile([P, PACK, F], BF16, align_bytes=256, name="%s_sb%d" % (name, b))
            nc.sync.dma_start(out=t[:], in_=rows(dram, b))
            for h in range(HALVES):
                halves[(name, b, h)] = t[:, :, h * W : (h + 1) * W]

        load_l(0)
        load_half(z1, "z1", 0)
        load_l(1)
        load_half(z0, "z0", 0)
        load_half(z1, "z1", 1)
        load_whole(z1, "z1", 1)
        load_half(z0, "z0", 1)
        load_whole(z0, "z0", 1)
        for b in range(2, B):
            load_whole(z1, "z1", b)
            load_whole(z0, "z0", b)
        older = {1: "z0", 2: "z1"}
        outs = {1: out_0, 2: out_1}

        state = {}
        doubled = []
        fence = const.tile([P, 1], U32)
        quantised = set()
        l_quantised = set()
        emptied = set()
        issued = [0]

        def order(si):
            return BY_HALF if si < EARLY else BY_ROW

        all_banks = [STEPS[si] + jh for si in range(len(STEPS)) for jh in order(si)]

        def cols(h):
            return slice(h * W, (h + 1) * W)

        def regroup(stage, b, h, shares):
            src = halves[("z1", b, h)] if stage == 1 else state[("z", 1, b)][:, :, cols(h)]
            if ("g", stage, b, h) not in state:
                g = grouped.tile([P, W, PACK], BF16, align_bytes=64, tag="g%d" % stage, name="g%d" % stage)
                state[("g", stage, b, h)] = g
            g = state[("g", stage, b, h)]
            for copy, first, count in shares:
                copy(
                    out=g[:, first : first + count, :].rearrange("p (c i) t -> p c t i", i=4),
                    in_=src[:, :, first : first + count].rearrange("p t (c i) -> p c t i", i=4),
                )

        def multiply_ready():
            while issued[0] < len(all_banks):
                n = issued[0]
                stage, b, j, h = all_banks[n]
                if j // 2 not in l_quantised or (stage, b, h) not in quantised or (n >= BANKS and n - BANKS not in emptied):
                    break
                c, s = state[("q", stage, b, h)]
                acc = psum.tile([P, W], F32, tag="bank", name="acc")
                nc.tensor.matmul_mx(
                    out=acc[:],
                    lhsT=l_codes[:, j * P : (j + 1) * P].bitcast(FP8X4),
                    lhsT_scale=l_scales[:, j * P : (j + 1) * P],
                    rhs=c[:].bitcast(FP8X4),
                    rhs_scale=s[:],
                    start=True,
                    stop=True,
                )
                state[("acc", stage, b, j, h)] = acc
                issued[0] = n + 1

        def quantise(stage, b, h):
            g = state[("g", stage, b, h)]
            c = codes.tile([P, W], U32, align_bytes=64, tag="c%d" % stage, name="c%d" % stage)
            s = codes.tile([P, W], U8, align_bytes=64, tag="s%d" % stage, name="s%d" % stage)
            nc.vector.quantize_mx(
                out=c[:].bitcast(FP8X4), scales=s[:], in_=g[:].rearrange("p w t -> p (w t)")
            )
            state[("q", stage, b, h)] = (c, s)
            quantised.add((stage, b, h))
            multiply_ready()

        def result(stage, b):
            if ("z", stage, b) not in state:
                z = results.tile([P, PACK, F], F32, align_bytes=256, tag="res%d" % stage, name="res%d" % stage)
                state[("z", stage, b)] = z
            return state[("z", stage, b)]

        def finish(stage, b, j, h):
            nc.vector.scalar_tensor_tensor(
                out=result(stage, b)[:, j, cols(h)],
                in0=state[("acc", stage, b, j, h)][:],
                scalar=2.0,
                in1=halves[(older[stage], b, h)][:, j, :],
                op0=MULT,
                op1=SUBTRACT,
            )

        def double(stage, b, j, h):
            nc.scalar.mul(out=result(stage, b)[:, j, cols(h)], in_=state[("acc", stage, b, j, h)][:], mul=2.0)
            doubled.append((stage, b, j, h))

        def subtract_doubled():
            for stage, b, j, h in doubled:
                z = result(stage, b)
                nc.gpsimd.tensor_tensor(
                    out=z[:, j, cols(h)], in0=z[:, j, cols(h)], in1=halves[(older[stage], b, h)][:, j, :], op=SUBTRACT
                )
            doubled.clear()

        def hold_gpsimd(stage, b, h):
            nc.gpsimd.tensor_copy(out=fence[:], in_=state[("q", stage, b, h)][0][:, 0:1])

        def store(stage, b, first, count):
            part = slice(first, first + count)
            nc.sync.dma_start(out=rows(outs[stage], b)[:, part, :], in_=state[("z", stage, b)][:, part, :])

        ident = const.tile([P, P], F32)
        make_identity(nc, ident[:])
        l_grouped = const.tile([P, PACK * N], BF16, align_bytes=64)
        l_grouped_words = l_grouped[:].bitcast(F32).rearrange("q (j p u) -> q j p u", j=PACK, u=2)
        l_codes = const.tile([P, N], U32, align_bytes=64)
        l_scales = const.tile([P, N], U8, align_bytes=64)

        def transpose_l(pair):
            l_words = l_rows[pair][:].bitcast(F32).rearrange("p j (q u) -> p j u q", u=2)
            l_t = psum.tile([P, 2, 2, P], F32, tag="bank")
            for a in range(2):
                for e in range(2):
                    nc.tensor.transpose(l_t[:, a, e, :], l_words[:, a, e, :], ident[:])
            nc.scalar.copy(
                out=l_grouped_words[:, 2 * pair : 2 * pair + 2, :, :],
                in_=l_t[:].rearrange("q a u p -> q a p u"),
            )

        def quantise_l(pair):
            part = slice(2 * pair * P, 2 * (pair + 1) * P)
            nc.vector.quantize_mx(
                out=l_codes[:, part].bitcast(FP8X4),
                scales=l_scales[:, part],
                in_=l_grouped[:, 2 * pair * P * PACK : 2 * (pair + 1) * P * PACK],
            )
            l_quantised.add(pair)
            multiply_ready()

        due = {}
        for si in range(len(STEPS)):
            if si == 0:
                places = (None, (0, PACK - 1))
            elif si < EARLY:
                places = ((si - 1, BANKS - 1), (si, 2))
            elif si == EARLY:
                places = ((si - 1, BANKS - 2), (si - 1, BANKS - 1))
            else:
                places = ((si - 1, BANKS - 3), (si - 1, BANKS - 2))
            for h in range(HALVES):
                due.setdefault(places[h], []).append(STEPS[si] + (h,))

        transpose_l(0)
        regroup(
            1, 0, 0, ((nc.vector.tensor_copy, 0, VECTOR_SHARE), (nc.scalar.copy, VECTOR_SHARE, W - VECTOR_SHARE))
        )
        quantise_l(0)
        transpose_l(1)
        quantise(1, 0, 0)
        quantise_l(1)
        regroup(1, 0, 1, ((nc.scalar.copy, VECTOR_SHARE_1, W - VECTOR_SHARE_1),))

        for si in range(len(STEPS)):
            stage, b = STEPS[si]
            for i in range(BANKS):
                j, h = order(si)[i]
                if si + 1 < len(STEPS) and i % PACK == 0:
                    regroup(STEPS[si + 1][0], STEPS[si + 1][1], i // PACK, ((nc.scalar.copy, 0, W),))
                if (si, i) == (0, 2):
                    regroup(1, 0, 1, ((nc.vector.tensor_copy, 0, VECTOR_SHARE_1),))
                for q in due.get((si, i), []):
                    quantise(q[0], q[1], q[2])
                    if doubled and q[2] == HALVES - 1:
                        hold_gpsimd(q[0], q[1], q[2])
                        subtract_doubled()
                if stage == 2 and i in BESIDE:
                    double(stage, b, j, h)
                    if si + 1 == len(STEPS):
                        subtract_doubled()
                else:
                    finish(stage, b, j, h)
                emptied.add(si * BANKS + i)
                if stage == 1:
                    if i == BANKS - 1:
                        store(stage, b, 0, PACK)
                elif j % 2 == 1 and h == HALVES - 1:
                    store(stage, b, j - 1, 2)
                multiply_ready()
